import numpy as np
import ml_dtypes


def mxq(x, axis, fmt="e4m3"):
    dtype, down = {"e4m3": (ml_dtypes.float8_e4m3fn, 7), "e5m2": (ml_dtypes.float8_e5m2, 14)}[fmt]
    v = np.moveaxis(np.asarray(x, np.float32).astype(ml_dtypes.bfloat16).astype(np.float64), axis, -1)
    blocks = v.reshape(v.shape[:-1] + (-1, 32))
    amax = np.abs(blocks).max(-1, keepdims=True)
    byte = np.maximum(np.where(amax > 0, np.frexp(amax)[1] - 1 + 127, 0) - down, 1)
    scale = np.exp2(byte - 127.0)
    codes = (blocks / scale).astype(np.float32).astype(dtype).astype(np.float64)
    return np.moveaxis((codes * scale).reshape(v.shape), -1, axis)


WIDE = False


def mx_kscale(k):
    if not WIDE:
        return np.ones(k)
    levels = np.array([10, -10, 5, -5, 0])
    if k % 512:
        return np.exp2(np.random.permutation(np.resize(levels, k // 32))).repeat(32)
    a = np.empty((k // 512, 16))
    for p in range(k // 512):
        a[p, :8] = np.random.permutation(np.resize(levels, 8))
        for g in range(8):
            far = levels[np.abs(levels - a[p, g]) >= 10]
            a[p, g + 8] = far[np.random.randint(len(far))]
    return np.exp2(a.ravel()).repeat(32)


BF16 = ml_dtypes.bfloat16


def bf(x):
    return np.asarray(x, np.float32).astype(BF16)


def f64(x):
    return np.asarray(x).astype(np.float64)


B, D, H = 1024, 512, 1024


def sigmoid(v):
    return 1.0 / (1.0 + np.exp(-v))


def setup_inputs():
    s = mx_kscale(D)
    return {"x": bf(np.random.standard_normal((B, D)) * s),
            "W_ih0": bf(np.random.standard_normal((4 * H, D)) * 1.5 / np.sqrt(D) / s[None, :]),
            "b_ih0": bf(np.random.standard_normal(4 * H) * 0.3),
            "b_hh0": bf(np.random.standard_normal(4 * H) * 0.3)}


def reference(x, W_ih0, b_ih0, b_hh0):
    w = f64(W_ih0)
    b = f64(b_ih0) + f64(b_hh0)
    xq = mxq(f64(x), 1, "e4m3")
    a_i = (xq @ mxq(w[:H].T, 0, "e4m3")) + b[:H]
    a_go = (xq @ mxq(w[2 * H:].T, 0, "e4m3")) + b[2 * H:]
    a_g, a_o = a_go[:, :H], a_go[:, H:]
    c = sigmoid(a_i) * np.tanh(a_g)
    return sigmoid(a_o) * np.tanh(c)

@@ -1,0 +1,308 @@
+from contextlib import ExitStack
+
+import concourse.mybir as mybir
+from concourse.masks import make_identity
+
+F32 = mybir.dt.float32
+BF16 = mybir.dt.bfloat16
+U32 = mybir.dt.uint32
+U8 = mybir.dt.uint8
+FP8X4 = mybir.dt.float8_e4m3fn_x4
+AF = mybir.ActivationFunctionType
+ALU = mybir.AluOpType
+
+P = 128
+B, D, H = 1024, 512, 1024
+FLOPS = 2 * B * D * 3 * H
+BYTES = B * D * 2 + 3 * H * D * 2 + 2 * 3 * H * 2 + B * H * 4
+
+NB = B // P
+NH = H // P
+GATE_ROW_TILE = (0, 16, 24)
+WARM = 5
+
+
+def tile_lstmbaseline_pa_kernel(tc, x, W_ih0, b_ih0, b_hh0, out):
+    nc = tc.nc
+    with ExitStack() as ctx:
+        keep = ctx.enter_context(tc.tile_pool(name="keep", bufs=1))
+        work = ctx.enter_context(tc.tile_pool(name="work", bufs=3))
+        psum = ctx.enter_context(tc.psum_pool(name="psum", bufs=1))
+        ctx.enter_context(tc.manual_schedule())
+
+        x_sb = keep.tile([P, NB * D], BF16, name="x_sb")
+        w_sb = keep.tile([P, 3 * NH * D], BF16, name="w_sb")
+        xq = keep.tile([P, B], U32, name="xq", align_bytes=64)
+        xs = keep.tile([P, B], U8, name="xs", align_bytes=64)
+        wq = keep.tile([P, 3 * H], U32, name="wq", align_bytes=64)
+        ws = keep.tile([P, 3 * H], U8, name="ws", align_bytes=64)
+        out_sb = keep.tile([P, NB, H], F32, name="out_sb")
+        ident = keep.tile([P, P], F32, name="ident")
+        bsum = keep.tile([P, P], F32, name="bsum")
+        bih = keep.tile([32, P], BF16, name="bih")
+        bhh = keep.tile([32, P], BF16, name="bhh")
+        bias_sb = keep.tile([P, 32], F32, name="bias_sb")
+        warm_in = keep.tile([P, 1], F32, name="warm_in")
+        warm_out = keep.tile([P, 1], F32, name="warm_out")
+
+        x_view = x.rearrange("(p t) k -> p (t k)", t=NB)
+        out_view = out.rearrange("(p t) h -> p t h", t=NB)
+        x_words = x_sb[:].bitcast(F32)
+        w_words = w_sb[:].bitcast(F32)
+
+        def bank(tag):
+            return psum.tile([P, 512], F32, name="ps_" + tag, tag=tag)
+
+        mx_count = [0]
+
+        def mx_bank():
+            tag = "m%d" % (mx_count[0] % 4)
+            mx_count[0] += 1
+            return bank(tag)
+
+        def load_x(pair):
+            cols = slice(pair * 2 * D, (pair + 1) * 2 * D)
+            nc.sync.dma_start(out=x_sb[:, cols], in_=x_view[:, cols])
+
+        def load_w(gi, ht, count):
+            slot = gi * NH + ht
+            row = (GATE_ROW_TILE[gi] + ht) * P
+            nc.sync.dma_start(
+                out=w_sb[:, slot * D : (slot + count) * D].rearrange("p (t k) -> p t k", t=count),
+                in_=W_ih0[row : row + count * P, :].rearrange("(t p) k -> p t k", p=P),
+            )
+
+        def job_words(job):
+            kind, a, b2 = job
+            if kind == "x":
+                return x_words, a * 2
+            return w_words, a * NH + 2 * b2
+
+        def prep_transpose(job, tag):
+            words, first = job_words(job)
+            ps = bank(tag)
+            for r in range(2):
+                for u in range(2):
+                    src = words[:, (first + r) * 256 + u : (first + r + 1) * 256 : 2]
+                    nc.tensor.transpose(ps[:, u * 256 + r * P : u * 256 + (r + 1) * P], src, ident[:])
+            return ps
+
+        def prep_copy(engine, ps):
+            grouped = work.tile([P, 1024], BF16, name="grouped", tag="grouped", bufs=4, align_bytes=64)
+            dst = grouped[:].bitcast(F32).rearrange("p (c u) -> p c u", u=2)
+            src = ps[:].rearrange("p (u c) -> p c u", u=2)
+            if engine == "v":
+                nc.vector.tensor_copy(out=dst, in_=src)
+            else:
+                nc.scalar.copy(out=dst, in_=src)
+            return grouped
+
+        def prep_quant(job, grouped):
+            kind, a, b2 = job
+            if kind == "x":
+                codes, scales, c0 = xq, xs, a * 256
+            else:
+                codes, scales, c0 = wq, ws, (a * NH + 2 * b2) * P
+            nc.vector.quantize_mx(
+                out=codes[:, c0 : c0 + 256].bitcast(FP8X4), scales=scales[:, c0 : c0 + 256], in_=grouped[:]
+            )
+
+        units = []
+        for hp in range(NH // 2):
+            for grp in range(2):
+                for ht in (2 * hp, 2 * hp + 1):
+                    units.append((ht, grp))
+        NU = len(units)
+        acts = {}
+        c_t = {}
+        c_ps = {}
+        o_ps = {}
+        th = {}
+
+        def mx_pass(n, gi, c0, c1):
+            ht, grp = units[n]
+            ps = mx_bank()
+            slot = gi * NH + ht
+            cols = slice(grp * 512 + c0, grp * 512 + c1)
+            nc.tensor.matmul_mx(
+                out=ps[:, 0 : c1 - c0],
+                lhsT=wq[:, slot * P : (slot + 1) * P].bitcast(FP8X4),
+                lhsT_scale=ws[:, slot * P : (slot + 1) * P],
+                rhs=xq[:, cols].bitcast(FP8X4),
+                rhs_scale=xs[:, cols],
+                start=True,
+                stop=True,
+            )
+            return ps
+
+        def act_gate(n, gi, ps, c0, c1):
+            ht, grp = units[n]
+            if (n, gi) not in acts:
+                acts[(n, gi)] = work.tile([P, 512], F32, name="gate%d" % gi, tag="gate%d" % gi)
+            col = GATE_ROW_TILE[gi] + ht
+            nc.scalar.activation(
+                out=acts[(n, gi)][:, c0:c1],
+                in_=ps[:, 0 : c1 - c0],
+                func=AF.Tanh if gi == 1 else AF.Sigmoid,
+                bias=bias_sb[:, col : col + 1],
+                scale=1.0,
+            )
+
+        def cmult(engine, n, c0, c1):
+            if n not in c_t:
+                c_t[n] = work.tile([P, 512], F32, name="c_t", tag="c_t")
+            engine.tensor_tensor(
+                out=c_t[n][:, c0:c1], in0=acts[(n, 0)][:, c0:c1], in1=acts[(n, 1)][:, c0:c1], op=ALU.mult
+            )
+
+        def back_transpose(src, ps, t0, t1):
+            for tl in range(t0, t1):
+                nc.tensor.transpose(
+                    ps[:, (tl - t0) * P : (tl - t0 + 1) * P], src[:, tl * P : (tl + 1) * P], ident[:]
+                )
+            return ps
+
+        def act_c(n, ps, c0, c1):
+            if n not in th:
+                th[n] = work.tile([P, 512], F32, name="th", tag="th")
+            nc.scalar.activation(out=th[n][:, c0:c1], in_=ps[:, 0 : c1 - c0], func=AF.Tanh)
+
+        def final(n, t0, t1):
+            ht, grp = units[n]
+            nc.vector.tensor_tensor(
+                out=out_sb[:, 4 * grp + t0 : 4 * grp + t1, ht * P : (ht + 1) * P],
+                in0=o_ps[n][:, t0 * P : t1 * P].rearrange("p (t m) -> p t m", m=P),
+                in1=th[n][:, t0 * P : t1 * P].rearrange("p (t m) -> p t m", m=P),
+                op=ALU.mult,
+            )
+
+        def store(t0, t1, h0, h1):
+            nc.sync.dma_start(out=out_view[:, t0:t1, h0:h1], in_=out_sb[:, t0:t1, h0:h1])
+
+        nc.scalar.dma_start(out=bih[:], in_=b_ih0.rearrange("(t p) -> t p", p=P))
+        nc.scalar.dma_start(out=bhh[:], in_=b_hh0.rearrange("(t p) -> t p", p=P))
+        load_w(0, 0, 1)
+        load_w(0, 1, 1)
+        load_x(0)
+        load_x(1)
+        load_w(1, 0, 2)
+        load_w(2, 0, 2)
+        load_x(2)
+        load_x(3)
+        for hp in range(1, NH // 2):
+            for gi in range(3):
+                load_w(gi, 2 * hp, 2)
+
+        make_identity(nc, ident[:])
+        nc.vector.memset(warm_in[:], 0.0)
+        nc.vector.memset(bsum[:], 0.0)
+        nc.scalar.activation(out=warm_out[:], in_=warm_in[:], func=AF.Sigmoid)
+        if WARM:
+            zeros = keep.tile([P, 512], BF16, name="zeros")
+            nc.vector.memset(zeros[:], 0.0)
+            ps_warm = bank("m3")
+
+        def dummy(count):
+            for k in range(count):
+                nc.tensor.matmul(out=ps_warm[:], lhsT=zeros[:, 0:P], rhs=zeros[:], start=True, stop=True)
+
+        dummy(WARM)
+
+        j_w = [("w", gi, 0) for gi in range(3)]
+        j_x = [("x", k, 0) for k in range(4)]
+        p_wi = prep_transpose(j_w[0], "o1")
+        dummy(1)
+        p_x0 = prep_transpose(j_x[0], "in0")
+        dummy(1)
+        p_x1 = prep_transpose(j_x[1], "o0")
+        dummy(1)
+        nc.vector.tensor_tensor(out=bsum[0:32, :], in0=bih[:], in1=bhh[:], op=ALU.add)
+        p_b = bank("c0")
+        nc.tensor.transpose(p_b[:, 0:P], bsum[:], ident[:])
+        g_wi = prep_copy("v", p_wi)
+        g_x0 = prep_copy("s", p_x0)
+        prep_quant(j_w[0], g_wi)
+        g_x1 = prep_copy("s", p_x1)
+        prep_quant(j_x[0], g_x0)
+        nc.vector.tensor_copy(out=bias_sb[:], in_=p_b[:, 0:32])
+        prep_quant(j_x[1], g_x1)
+        p_wg = prep_transpose(j_w[1], "o1")
+        g_wg = prep_copy("s", p_wg)
+        ia = [mx_pass(0, 0, 0, 256), mx_pass(1, 0, 0, 256)]
+        p_wo = prep_transpose(j_w[2], "in0")
+        ib = [mx_pass(0, 0, 256, 512), mx_pass(1, 0, 256, 512)]
+        act_gate(0, 0, ia[0], 0, 256)
+        act_gate(1, 0, ia[1], 0, 256)
+        act_gate(0, 0, ib[0], 256, 512)
+        act_gate(1, 0, ib[1], 256, 512)
+        prep_quant(j_w[1], g_wg)
+        g_wo = prep_copy("v", p_wo)
+        prep_quant(j_w[2], g_wo)
+        gg = [mx_pass(0, 1, 0, 512), mx_pass(1, 1, 0, 512)]
+        p_x2 = prep_transpose(j_x[2], "o0")
+        act_gate(0, 1, gg[0], 0, 512)
+        act_gate(1, 1, gg[1], 0, 512)
+        cmult(nc.gpsimd, 0, 0, 512)
+        cmult(nc.gpsimd, 1, 0, 512)
+        oo = [mx_pass(0, 2, 0, 512), mx_pass(1, 2, 0, 512)]
+        p_x3 = prep_transpose(j_x[3], "o1")
+        act_gate(0, 2, oo[0], 0, 512)
+        act_gate(1, 2, oo[1], 0, 512)
+        g_x2 = prep_copy("v", p_x2)
+        prep_quant(j_x[2], g_x2)
+        g_x3 = prep_copy("v", p_x3)
+        prep_quant(j_x[3], g_x3)
+        o_ps[0] = back_transpose(acts[(0, 2)], bank("o0"), 0, 4)
+        c_ps[0] = back_transpose(c_t[0], bank("c0"), 0, 4)
+        j_wi1 = ("w", 0, 1)
+        p_wi1 = prep_transpose(j_wi1, "in0")
+        act_c(0, c_ps[0], 0, 512)
+        nxt = [mx_pass(2, gi, 0, 512) for gi in range(3)]
+        pending = [(j_wi1, prep_copy("v", p_wi1))]
+
+        jobs = {2: [(("w", 1, 1), "in0"), (("w", 2, 1), "o0")]}
+        for hp in (2, 3):
+            for gi in range(3):
+                jobs[4 * hp - 4 + gi] = [(("w", gi, hp), "in0")]
+
+        for n in range(2, NU):
+            for job, grouped in pending:
+                prep_quant(job, grouped)
+            pending = []
+            final(n - 2, 0, 4)
+            ht, grp = units[n - 2]
+            if ht % 2 == 1:
+                store(4 * grp, 4 * grp + 4, (ht - 1) * P, (ht + 1) * P)
+            o_ps[n - 1] = back_transpose(acts[(n - 1, 2)], bank("o%d" % ((n - 1) % 2)), 0, 4)
+            banks = [(job, prep_transpose(job, tag)) for job, tag in jobs.get(n, [])]
+            c_ps[n - 1] = back_transpose(c_t[n - 1], bank("c0"), 0, 4)
+            cur = nxt
+            act_gate(n, 0, cur[0], 0, 512)
+            act_gate(n, 1, cur[1], 0, 512)
+            if n + 1 < NU:
+                nxt = [mx_pass(n + 1, gi, 0, 512) for gi in range(3)]
+            act_gate(n, 2, cur[2], 0, 512)
+            act_c(n - 1, c_ps[n - 1], 0, 512)
+            if n < NU - 2:
+                cmult(nc.gpsimd, n, 0, 512)
+            elif n == NU - 2:
+                cmult(nc.vector, n, 0, 512)
+            else:
+                cmult(nc.vector, n, 0, 256)
+                cmult(nc.vector, n, 256, 512)
+            for job, ps in banks:
+                pending.append((job, prep_copy("v", ps)))
+
+        last = NU - 1
+        ht, grp = units[last - 1]
+        final(last - 1, 0, 4)
+        store(4 * grp, 4 * grp + 4, ht * P, (ht + 1) * P)
+        ht, grp = units[last]
+        c_a = back_transpose(c_t[last], bank("in0"), 0, 2)
+        c_b = back_transpose(c_t[last], mx_bank(), 2, 4)
+        o_ps[last] = back_transpose(acts[(last, 2)], bank("o%d" % (last % 2)), 0, 4)
+        act_c(last, c_a, 0, 256)
+        act_c(last, c_b, 256, 512)
+        for t0 in (0, 2):
+            final(last, t0, t0 + 2)
+            store(4 * grp + t0, 4 * grp + t0 + 2, ht * P, (ht + 1) * P)

@@ -19,7 +19,7 @@ BYTES = B * D * 2 + 3 * H * D * 2 + 2 * 3 * H * 2 + B * H * 4
 NB = B // P
 NH = H // P
 GATE_ROW_TILE = (0, 16, 24)
-WARM = 5
+WARM = 18
 
 
 def tile_lstmbaseline_pa_kernel(tc, x, W_ih0, b_ih0, b_hh0, out):
@@ -56,7 +56,7 @@ def tile_lstmbaseline_pa_kernel(tc, x, W_ih0, b_ih0, b_hh0, out):
         mx_count = [0]
 
         def mx_bank():
-            tag = "m%d" % (mx_count[0] % 4)
+            tag = "m%d" % (mx_count[0] % 3)
             mx_count[0] += 1
             return bank(tag)
 
@@ -119,9 +119,9 @@ def tile_lstmbaseline_pa_kernel(tc, x, W_ih0, b_ih0, b_hh0, out):
         o_ps = {}
         th = {}
 
-        def mx_pass(n, gi, c0, c1):
+        def mx_pass(n, gi, c0, c1, ps=None):
             ht, grp = units[n]
-            ps = mx_bank()
+            ps = mx_bank() if ps is None else ps
             slot = gi * NH + ht
             cols = slice(grp * 512 + c0, grp * 512 + c1)
             nc.tensor.matmul_mx(
@@ -135,14 +135,15 @@ def tile_lstmbaseline_pa_kernel(tc, x, W_ih0, b_ih0, b_hh0, out):
             )
             return ps
 
-        def act_gate(n, gi, ps, c0, c1):
+        def act_gate(n, gi, ps, c0, c1, first=None):
+            first = 0 if first is None else first
             ht, grp = units[n]
             if (n, gi) not in acts:
                 acts[(n, gi)] = work.tile([P, 512], F32, name="gate%d" % gi, tag="gate%d" % gi)
             col = GATE_ROW_TILE[gi] + ht
             nc.scalar.activation(
                 out=acts[(n, gi)][:, c0:c1],
-                in_=ps[:, 0 : c1 - c0],
+                in_=ps[:, first : first + c1 - c0],
                 func=AF.Tanh if gi == 1 else AF.Sigmoid,
                 bias=bias_sb[:, col : col + 1],
                 scale=1.0,
@@ -162,16 +163,17 @@ def tile_lstmbaseline_pa_kernel(tc, x, W_ih0, b_ih0, b_hh0, out):
                 )
             return ps
 
-        def act_c(n, ps, c0, c1):
+        def act_c(n, ps, c0, c1, first=0):
             if n not in th:
                 th[n] = work.tile([P, 512], F32, name="th", tag="th")
-            nc.scalar.activation(out=th[n][:, c0:c1], in_=ps[:, 0 : c1 - c0], func=AF.Tanh)
+            nc.scalar.activation(out=th[n][:, c0:c1], in_=ps[:, first : first + c1 - c0], func=AF.Tanh)
 
-        def final(n, t0, t1):
+        def final(n, t0, t1, ps=None, first=0):
             ht, grp = units[n]
+            ps = o_ps[n] if ps is None else ps
             nc.vector.tensor_tensor(
                 out=out_sb[:, 4 * grp + t0 : 4 * grp + t1, ht * P : (ht + 1) * P],
-                in0=o_ps[n][:, t0 * P : t1 * P].rearrange("p (t m) -> p t m", m=P),
+                in0=ps[:, (t0 - first) * P : (t1 - first) * P].rearrange("p (t m) -> p t m", m=P),
                 in1=th[n][:, t0 * P : t1 * P].rearrange("p (t m) -> p t m", m=P),
                 op=ALU.mult,
             )
@@ -193,44 +195,42 @@ def tile_lstmbaseline_pa_kernel(tc, x, W_ih0, b_ih0, b_hh0, out):
             for gi in range(3):
                 load_w(gi, 2 * hp, 2)
 
-        make_identity(nc, ident[:])
+        zeros = keep.tile([P, P], BF16, name="zeros")
+        nc.vector.memset(zeros[:], 0.0)
         nc.vector.memset(warm_in[:], 0.0)
         nc.vector.memset(bsum[:], 0.0)
+        make_identity(nc, ident[:])
         nc.scalar.activation(out=warm_out[:], in_=warm_in[:], func=AF.Sigmoid)
-        if WARM:
-            zeros = keep.tile([P, 512], BF16, name="zeros")
-            nc.vector.memset(zeros[:], 0.0)
-            ps_warm = bank("m3")
+        ps_warm = bank("in1")
 
         def dummy(count):
             for k in range(count):
-                nc.tensor.matmul(out=ps_warm[:], lhsT=zeros[:, 0:P], rhs=zeros[:], start=True, stop=True)
+                nc.tensor.matmul(out=ps_warm[:, 0:P], lhsT=zeros[:], rhs=zeros[:], start=True, stop=True)
 
         dummy(WARM)
 
         j_w = [("w", gi, 0) for gi in range(3)]
         j_x = [("x", k, 0) for k in range(4)]
         p_wi = prep_transpose(j_w[0], "o1")
-        dummy(1)
-        p_x0 = prep_transpose(j_x[0], "in0")
-        dummy(1)
-        p_x1 = prep_transpose(j_x[1], "o0")
-        dummy(1)
         nc.vector.tensor_tensor(out=bsum[0:32, :], in0=bih[:], in1=bhh[:], op=ALU.add)
         p_b = bank("c0")
         nc.tensor.transpose(p_b[:, 0:P], bsum[:], ident[:])
+        p_x0 = prep_transpose(j_x[0], "in0")
+        dummy(4)
+        p_x1 = prep_transpose(j_x[1], "o0")
+        dummy(4)
         g_wi = prep_copy("v", p_wi)
+        nc.vector.tensor_copy(out=bias_sb[:], in_=p_b[:, 0:32])
         g_x0 = prep_copy("s", p_x0)
         prep_quant(j_w[0], g_wi)
         g_x1 = prep_copy("s", p_x1)
         prep_quant(j_x[0], g_x0)
-        nc.vector.tensor_copy(out=bias_sb[:], in_=p_b[:, 0:32])
         prep_quant(j_x[1], g_x1)
         p_wg = prep_transpose(j_w[1], "o1")
         g_wg = prep_copy("s", p_wg)
         ia = [mx_pass(0, 0, 0, 256), mx_pass(1, 0, 0, 256)]
+        ib = [mx_pass(0, 0, 256, 512), mx_pass(1, 0, 256, 512, bank("c0"))]
         p_wo = prep_transpose(j_w[2], "in0")
-        ib = [mx_pass(0, 0, 256, 512), mx_pass(1, 0, 256, 512)]
         act_gate(0, 0, ia[0], 0, 256)
         act_gate(1, 0, ia[1], 0, 256)
         act_gate(0, 0, ib[0], 256, 512)
@@ -239,7 +239,7 @@ def tile_lstmbaseline_pa_kernel(tc, x, W_ih0, b_ih0, b_hh0, out):
         g_wo = prep_copy("v", p_wo)
         prep_quant(j_w[2], g_wo)
         gg = [mx_pass(0, 1, 0, 512), mx_pass(1, 1, 0, 512)]
-        p_x2 = prep_transpose(j_x[2], "o0")
+        p_x2 = prep_transpose(j_x[2], "in1")
         act_gate(0, 1, gg[0], 0, 512)
         act_gate(1, 1, gg[1], 0, 512)
         cmult(nc.gpsimd, 0, 0, 512)
@@ -252,20 +252,21 @@ def tile_lstmbaseline_pa_kernel(tc, x, W_ih0, b_ih0, b_hh0, out):
         prep_quant(j_x[2], g_x2)
         g_x3 = prep_copy("v", p_x3)
         prep_quant(j_x[3], g_x3)
-        o_ps[0] = back_transpose(acts[(0, 2)], bank("o0"), 0, 4)
         c_ps[0] = back_transpose(c_t[0], bank("c0"), 0, 4)
+        nxt = [mx_pass(2, gi, 0, 512) for gi in range(3)]
+        act_c(0, c_ps[0], 0, 512)
+        c_ps[1] = back_transpose(c_t[1], bank("c0"), 0, 4)
         j_wi1 = ("w", 0, 1)
         p_wi1 = prep_transpose(j_wi1, "in0")
-        act_c(0, c_ps[0], 0, 512)
-        nxt = [mx_pass(2, gi, 0, 512) for gi in range(3)]
+        o_ps[0] = back_transpose(acts[(0, 2)], bank("o0"), 0, 4)
         pending = [(j_wi1, prep_copy("v", p_wi1))]
 
-        jobs = {2: [(("w", 1, 1), "in0"), (("w", 2, 1), "o0")]}
+        jobs = {}
         for hp in (2, 3):
             for gi in range(3):
-                jobs[4 * hp - 4 + gi] = [(("w", gi, hp), "in0")]
+                jobs[4 * hp - 4 + gi] = [(("w", gi, hp), "in%d" % (gi % 2))]
 
-        for n in range(2, NU):
+        for n in range(2, NU - 2):
             for job, grouped in pending:
                 prep_quant(job, grouped)
             pending = []
@@ -273,36 +274,65 @@ def tile_lstmbaseline_pa_kernel(tc, x, W_ih0, b_ih0, b_hh0, out):
             ht, grp = units[n - 2]
             if ht % 2 == 1:
                 store(4 * grp, 4 * grp + 4, (ht - 1) * P, (ht + 1) * P)
-            o_ps[n - 1] = back_transpose(acts[(n - 1, 2)], bank("o%d" % ((n - 1) % 2)), 0, 4)
-            banks = [(job, prep_transpose(job, tag)) for job, tag in jobs.get(n, [])]
-            c_ps[n - 1] = back_transpose(c_t[n - 1], bank("c0"), 0, 4)
+            banks = []
+            if n > 2:
+                o_ps[n - 1] = back_transpose(acts[(n - 1, 2)], bank("o%d" % ((n - 1) % 2)), 0, 4)
+                for job, tag in jobs.get(n, []):
+                    banks.append((job, prep_transpose(job, tag)))
+                c_ps[n - 1] = back_transpose(c_t[n - 1], bank("c0"), 0, 4)
+            else:
+                banks.append((("w", 1, 1), prep_transpose(("w", 1, 1), "in1")))
             cur = nxt
             act_gate(n, 0, cur[0], 0, 512)
             act_gate(n, 1, cur[1], 0, 512)
-            if n + 1 < NU:
-                nxt = [mx_pass(n + 1, gi, 0, 512) for gi in range(3)]
+            nxt = [mx_pass(n + 1, gi, 0, 512) for gi in range(3)]
+            if n == 2:
+                o_ps[1] = back_transpose(acts[(1, 2)], bank("o1"), 0, 4)
+                banks.append((("w", 2, 1), prep_transpose(("w", 2, 1), "in0")))
             act_gate(n, 2, cur[2], 0, 512)
             act_c(n - 1, c_ps[n - 1], 0, 512)
-            if n < NU - 2:
-                cmult(nc.gpsimd, n, 0, 512)
-            elif n == NU - 2:
-                cmult(nc.vector, n, 0, 512)
-            else:
-                cmult(nc.vector, n, 0, 256)
-                cmult(nc.vector, n, 256, 512)
+            cmult(nc.gpsimd, n, 0, 512)
             for job, ps in banks:
                 pending.append((job, prep_copy("v", ps)))
 
-        last = NU - 1
-        ht, grp = units[last - 1]
-        final(last - 1, 0, 4)
+        a, z = NU - 2, NU - 1
+        final(a - 2, 0, 4)
+        ht, grp = units[a - 2]
         store(4 * grp, 4 * grp + 4, ht * P, (ht + 1) * P)
-        ht, grp = units[last]
-        c_a = back_transpose(c_t[last], bank("in0"), 0, 2)
-        c_b = back_transpose(c_t[last], mx_bank(), 2, 4)
-        o_ps[last] = back_transpose(acts[(last, 2)], bank("o%d" % (last % 2)), 0, 4)
-        act_c(last, c_a, 0, 256)
-        act_c(last, c_b, 256, 512)
-        for t0 in (0, 2):
-            final(last, t0, t0 + 2)
-            store(4 * grp + t0, 4 * grp + t0 + 2, ht * P, (ht + 1) * P)
+        o_ps[a - 1] = back_transpose(acts[(a - 1, 2)], bank("o%d" % ((a - 1) % 2)), 0, 4)
+        c_ps[a - 1] = back_transpose(c_t[a - 1], bank("c0"), 0, 4)
+        act_gate(a, 0, nxt[0], 0, 512)
+        act_gate(a, 1, nxt[1], 0, 512)
+        cmult(nc.gpsimd, a, 0, 512)
+        zi = mx_pass(z, 0, 0, 512)
+        zg = mx_pass(z, 1, 0, 512)
+        zo = mx_pass(z, 2, 0, 512, bank("in1"))
+        act_c(a - 1, c_ps[a - 1], 0, 512)
+        act_gate(z, 0, zi, 0, 512)
+        act_gate(z, 1, zg, 0, 256)
+        act_gate(z, 1, zg, 256, 512, 256)
+        act_gate(a, 2, nxt[2], 0, 512)
+        final(a - 1, 0, 4)
+        ht, grp = units[a - 1]
+        store(4 * grp, 4 * grp + 4, ht * P, (ht + 1) * P)
+        cmult(nc.vector, z, 0, 256)
+        cmult(nc.vector, z, 256, 512)
+        c_ps[a] = back_transpose(c_t[a], bank("in0"), 0, 4)
+        c_lo = back_transpose(c_t[z], bank("m0"), 0, 2)
+        c_hi = back_transpose(c_t[z], bank("m1"), 2, 4)
+        o_ps[a] = back_transpose(acts[(a, 2)], bank("o%d" % (a % 2)), 0, 4)
+        act_c(a, c_ps[a], 0, 512)
+        act_gate(z, 2, zo, 0, 256)
+        act_gate(z, 2, zo, 256, 512, 256)
+        final(a, 0, 4)
+        ht, grp = units[a]
+        store(4 * grp, 4 * grp + 4, ht * P, (ht + 1) * P)
+        o_lo = back_transpose(acts[(z, 2)], bank("o%d" % (z % 2)), 0, 2)
+        o_hi = back_transpose(acts[(z, 2)], bank("m2"), 2, 4)
+        ht, grp = units[z]
+        act_c(z, c_lo, 0, 256)
+        act_c(z, c_hi, 256, 384)
+        act_c(z, c_hi, 384, 512, 128)
+        for t0, t1, ps, first in ((0, 2, o_lo, 0), (2, 3, o_hi, 2), (3, 4, o_hi, 2)):
+            final(z, t0, t1, ps, first)
+            store(4 * grp + t0, 4 * grp + t1, ht * P, (ht + 1) * P)

@@ -19,7 +19,7 @@ BYTES = B * D * 2 + 3 * H * D * 2 + 2 * 3 * H * 2 + B * H * 4
 NB = B // P
 NH = H // P
 GATE_ROW_TILE = (0, 16, 24)
-WARM = 18
+WARM = 5
 
 
 def tile_lstmbaseline_pa_kernel(tc, x, W_ih0, b_ih0, b_hh0, out):
@@ -56,7 +56,7 @@ def tile_lstmbaseline_pa_kernel(tc, x, W_ih0, b_ih0, b_hh0, out):
         mx_count = [0]
 
         def mx_bank():
-            tag = "m%d" % (mx_count[0] % 3)
+            tag = "m%d" % (mx_count[0] % 4)
             mx_count[0] += 1
             return bank(tag)
 
@@ -139,7 +139,7 @@ def tile_lstmbaseline_pa_kernel(tc, x, W_ih0, b_ih0, b_hh0, out):
             first = 0 if first is None else first
             ht, grp = units[n]
             if (n, gi) not in acts:
-                acts[(n, gi)] = work.tile([P, 512], F32, name="gate%d" % gi, tag="gate%d" % gi)
+                acts[(n, gi)] = work.tile([P, 512], F32, name="gate%d" % gi, tag="gate%d" % gi, bufs=4)
             col = GATE_ROW_TILE[gi] + ht
             nc.scalar.activation(
                 out=acts[(n, gi)][:, c0:c1],
@@ -151,7 +151,7 @@ def tile_lstmbaseline_pa_kernel(tc, x, W_ih0, b_ih0, b_hh0, out):
 
         def cmult(engine, n, c0, c1):
             if n not in c_t:
-                c_t[n] = work.tile([P, 512], F32, name="c_t", tag="c_t")
+                c_t[n] = work.tile([P, 512], F32, name="c_t", tag="c_t", bufs=4)
             engine.tensor_tensor(
                 out=c_t[n][:, c0:c1], in0=acts[(n, 0)][:, c0:c1], in1=acts[(n, 1)][:, c0:c1], op=ALU.mult
             )
@@ -195,144 +195,144 @@ def tile_lstmbaseline_pa_kernel(tc, x, W_ih0, b_ih0, b_hh0, out):
             for gi in range(3):
                 load_w(gi, 2 * hp, 2)
 
-        zeros = keep.tile([P, P], BF16, name="zeros")
+        zeros = keep.tile([P, 512], BF16, name="zeros")
         nc.vector.memset(zeros[:], 0.0)
         nc.vector.memset(warm_in[:], 0.0)
         nc.vector.memset(bsum[:], 0.0)
         make_identity(nc, ident[:])
         nc.scalar.activation(out=warm_out[:], in_=warm_in[:], func=AF.Sigmoid)
-        ps_warm = bank("in1")
+        ps_warm = bank("m3")
 
         def dummy(count):
             for k in range(count):
-                nc.tensor.matmul(out=ps_warm[:, 0:P], lhsT=zeros[:], rhs=zeros[:], start=True, stop=True)
+                nc.tensor.matmul(out=ps_warm[:], lhsT=zeros[:, 0:P], rhs=zeros[:], start=True, stop=True)
 
         dummy(WARM)
 
         j_w = [("w", gi, 0) for gi in range(3)]
+        j_v = [("w", gi, 1) for gi in range(3)]
         j_x = [("x", k, 0) for k in range(4)]
         p_wi = prep_transpose(j_w[0], "o1")
         nc.vector.tensor_tensor(out=bsum[0:32, :], in0=bih[:], in1=bhh[:], op=ALU.add)
         p_b = bank("c0")
         nc.tensor.transpose(p_b[:, 0:P], bsum[:], ident[:])
         p_x0 = prep_transpose(j_x[0], "in0")
-        dummy(4)
+        dummy(1)
         p_x1 = prep_transpose(j_x[1], "o0")
-        dummy(4)
+        dummy(1)
         g_wi = prep_copy("v", p_wi)
         nc.vector.tensor_copy(out=bias_sb[:], in_=p_b[:, 0:32])
         g_x0 = prep_copy("s", p_x0)
         prep_quant(j_w[0], g_wi)
         g_x1 = prep_copy("s", p_x1)
         prep_quant(j_x[0], g_x0)
-        prep_quant(j_x[1], g_x1)
         p_wg = prep_transpose(j_w[1], "o1")
         g_wg = prep_copy("s", p_wg)
-        ia = [mx_pass(0, 0, 0, 256), mx_pass(1, 0, 0, 256)]
-        ib = [mx_pass(0, 0, 256, 512), mx_pass(1, 0, 256, 512, bank("c0"))]
         p_wo = prep_transpose(j_w[2], "in0")
+        ia = [mx_pass(0, 0, 0, 256), mx_pass(1, 0, 0, 256)]
+        prep_quant(j_x[1], g_x1)
+        g_wo = prep_copy("v", p_wo)
+        ib = [mx_pass(0, 0, 256, 512), mx_pass(1, 0, 256, 512)]
         act_gate(0, 0, ia[0], 0, 256)
         act_gate(1, 0, ia[1], 0, 256)
         act_gate(0, 0, ib[0], 256, 512)
         act_gate(1, 0, ib[1], 256, 512)
+        p_x2 = prep_transpose(j_x[2], "o0")
         prep_quant(j_w[1], g_wg)
-        g_wo = prep_copy("v", p_wo)
+        g_x2 = prep_copy("v", p_x2)
         prep_quant(j_w[2], g_wo)
         gg = [mx_pass(0, 1, 0, 512), mx_pass(1, 1, 0, 512)]
-        p_x2 = prep_transpose(j_x[2], "in1")
+        p_x3 = prep_transpose(j_x[3], "c0")
         act_gate(0, 1, gg[0], 0, 512)
         act_gate(1, 1, gg[1], 0, 512)
         cmult(nc.gpsimd, 0, 0, 512)
         cmult(nc.gpsimd, 1, 0, 512)
+        g_x3 = prep_copy("v", p_x3)
+        prep_quant(j_x[2], g_x2)
         oo = [mx_pass(0, 2, 0, 512), mx_pass(1, 2, 0, 512)]
-        p_x3 = prep_transpose(j_x[3], "o1")
+        prep_quant(j_x[3], g_x3)
+        p_v = prep_transpose(j_v[0], "o1")
+        g_v = prep_copy("v", p_v)
         act_gate(0, 2, oo[0], 0, 512)
         act_gate(1, 2, oo[1], 0, 512)
-        g_x2 = prep_copy("v", p_x2)
-        prep_quant(j_x[2], g_x2)
-        g_x3 = prep_copy("v", p_x3)
-        prep_quant(j_x[3], g_x3)
-        c_ps[0] = back_transpose(c_t[0], bank("c0"), 0, 4)
         nxt = [mx_pass(2, gi, 0, 512) for gi in range(3)]
-        act_c(0, c_ps[0], 0, 512)
-        c_ps[1] = back_transpose(c_t[1], bank("c0"), 0, 4)
-        j_wi1 = ("w", 0, 1)
-        p_wi1 = prep_transpose(j_wi1, "in0")
-        o_ps[0] = back_transpose(acts[(0, 2)], bank("o0"), 0, 4)
-        pending = [(j_wi1, prep_copy("v", p_wi1))]
+        pending = [(j_v[0], g_v)]
 
-        jobs = {}
+        jobs = {2: [(j_v[1], "in0"), (j_v[2], "o1")]}
         for hp in (2, 3):
             for gi in range(3):
-                jobs[4 * hp - 4 + gi] = [(("w", gi, hp), "in%d" % (gi % 2))]
+                jobs[4 * hp - 4 + gi] = [(("w", gi, hp), "in0")]
 
         for n in range(2, NU - 2):
-            for job, grouped in pending:
-                prep_quant(job, grouped)
-            pending = []
-            final(n - 2, 0, 4)
-            ht, grp = units[n - 2]
-            if ht % 2 == 1:
-                store(4 * grp, 4 * grp + 4, (ht - 1) * P, (ht + 1) * P)
-            banks = []
+            k = n - 2
             if n > 2:
-                o_ps[n - 1] = back_transpose(acts[(n - 1, 2)], bank("o%d" % ((n - 1) % 2)), 0, 4)
-                for job, tag in jobs.get(n, []):
-                    banks.append((job, prep_transpose(job, tag)))
-                c_ps[n - 1] = back_transpose(c_t[n - 1], bank("c0"), 0, 4)
-            else:
-                banks.append((("w", 1, 1), prep_transpose(("w", 1, 1), "in1")))
+                for job, grouped in pending:
+                    prep_quant(job, grouped)
+                pending = []
+                if k > 0:
+                    final(k - 1, 0, 4)
+                    ht, grp = units[k - 1]
+                    if ht % 2 == 1:
+                        store(4 * grp, 4 * grp + 4, (ht - 1) * P, (ht + 1) * P)
+            o_ps[k] = back_transpose(acts[(k, 2)], bank("o%d" % (k % 2)), 0, 4)
+            c_ps[k] = back_transpose(c_t[k], bank("c0"), 0, 4)
+            banks = [(job, prep_transpose(job, tag)) for job, tag in jobs.get(n, [])]
             cur = nxt
             act_gate(n, 0, cur[0], 0, 512)
             act_gate(n, 1, cur[1], 0, 512)
             nxt = [mx_pass(n + 1, gi, 0, 512) for gi in range(3)]
-            if n == 2:
-                o_ps[1] = back_transpose(acts[(1, 2)], bank("o1"), 0, 4)
-                banks.append((("w", 2, 1), prep_transpose(("w", 2, 1), "in0")))
             act_gate(n, 2, cur[2], 0, 512)
-            act_c(n - 1, c_ps[n - 1], 0, 512)
+            act_c(k, c_ps[k], 0, 512)
             cmult(nc.gpsimd, n, 0, 512)
             for job, ps in banks:
-                pending.append((job, prep_copy("v", ps)))
+                grouped = prep_copy("v", ps)
+                if n == 2:
+                    prep_quant(*pending.pop(0))
+                pending.append((job, grouped))
 
         a, z = NU - 2, NU - 1
-        final(a - 2, 0, 4)
-        ht, grp = units[a - 2]
-        store(4 * grp, 4 * grp + 4, ht * P, (ht + 1) * P)
-        o_ps[a - 1] = back_transpose(acts[(a - 1, 2)], bank("o%d" % ((a - 1) % 2)), 0, 4)
-        c_ps[a - 1] = back_transpose(c_t[a - 1], bank("c0"), 0, 4)
+
+        def store_unit(n, t0, t1):
+            ht, grp = units[n]
+            store(4 * grp + t0, 4 * grp + t1, ht * P, (ht + 1) * P)
+
+        final(a - 3, 0, 4)
+        ht, grp = units[a - 3]
+        store(4 * grp, 4 * grp + 4, (ht - 1) * P, (ht + 1) * P)
+        o_ps[a - 2] = back_transpose(acts[(a - 2, 2)], bank("o%d" % ((a - 2) % 2)), 0, 4)
+        c_ps[a - 2] = back_transpose(c_t[a - 2], bank("c0"), 0, 4)
         act_gate(a, 0, nxt[0], 0, 512)
         act_gate(a, 1, nxt[1], 0, 512)
         cmult(nc.gpsimd, a, 0, 512)
-        zi = mx_pass(z, 0, 0, 512)
-        zg = mx_pass(z, 1, 0, 512)
-        zo = mx_pass(z, 2, 0, 512, bank("in1"))
+        zz = [mx_pass(z, gi, 0, 512) for gi in range(3)]
+        act_c(a - 2, c_ps[a - 2], 0, 512)
+        c_ps[a - 1] = back_transpose(c_t[a - 1], bank("in0"), 0, 4)
+        o_ps[a - 1] = back_transpose(acts[(a - 1, 2)], bank("o%d" % ((a - 1) % 2)), 0, 4)
+        act_gate(z, 0, zz[0], 0, 512)
+        act_gate(z, 1, zz[1], 0, 256)
+        act_gate(z, 1, zz[1], 256, 512, 256)
         act_c(a - 1, c_ps[a - 1], 0, 512)
-        act_gate(z, 0, zi, 0, 512)
-        act_gate(z, 1, zg, 0, 256)
-        act_gate(z, 1, zg, 256, 512, 256)
         act_gate(a, 2, nxt[2], 0, 512)
-        final(a - 1, 0, 4)
-        ht, grp = units[a - 1]
-        store(4 * grp, 4 * grp + 4, ht * P, (ht + 1) * P)
+        final(a - 2, 0, 4)
+        store_unit(a - 2, 0, 4)
         cmult(nc.vector, z, 0, 256)
         cmult(nc.vector, z, 256, 512)
-        c_ps[a] = back_transpose(c_t[a], bank("in0"), 0, 4)
-        c_lo = back_transpose(c_t[z], bank("m0"), 0, 2)
-        c_hi = back_transpose(c_t[z], bank("m1"), 2, 4)
+        final(a - 1, 0, 4)
+        store_unit(a - 1, 0, 4)
+        c_ps[a] = back_transpose(c_t[a], bank("c0"), 0, 4)
+        c_lo = back_transpose(c_t[z], bank("m3"), 0, 2)
+        c_hi = back_transpose(c_t[z], bank("m0"), 2, 4)
         o_ps[a] = back_transpose(acts[(a, 2)], bank("o%d" % (a % 2)), 0, 4)
         act_c(a, c_ps[a], 0, 512)
-        act_gate(z, 2, zo, 0, 256)
-        act_gate(z, 2, zo, 256, 512, 256)
+        act_gate(z, 2, zz[2], 0, 256)
+        act_gate(z, 2, zz[2], 256, 512, 256)
         final(a, 0, 4)
-        ht, grp = units[a]
-        store(4 * grp, 4 * grp + 4, ht * P, (ht + 1) * P)
-        o_lo = back_transpose(acts[(z, 2)], bank("o%d" % (z % 2)), 0, 2)
+        store_unit(a, 0, 4)
+        o_lo = back_transpose(acts[(z, 2)], bank("in0"), 0, 2)
         o_hi = back_transpose(acts[(z, 2)], bank("m2"), 2, 4)
-        ht, grp = units[z]
         act_c(z, c_lo, 0, 256)
         act_c(z, c_hi, 256, 384)
         act_c(z, c_hi, 384, 512, 128)
         for t0, t1, ps, first in ((0, 2, o_lo, 0), (2, 3, o_hi, 2), (3, 4, o_hi, 2)):
             final(z, t0, t1, ps, first)
-            store(4 * grp + t0, 4 * grp + t1, ht * P, (ht + 1) * P)
+            store_unit(z, t0, t1)

@@ -19,6 +19,8 @@ BYTES = B * D * 2 + 3 * H * D * 2 + 2 * 3 * H * 2 + B * H * 4
 NB = B // P
 NH = H // P
 GATE_ROW_TILE = (0, 16, 24)
+BLOCK_HP = (0, 1, 2)
+BLOCK_PAIRS = (0, 1, 2, 3, 4, 5)
 WARM = 5
 
 
@@ -38,15 +40,17 @@ def tile_lstmbaseline_pa_kernel(tc, x, W_ih0, b_ih0, b_hh0, out):
         ws = keep.tile([P, 3 * H], U8, name="ws", align_bytes=64)
         out_sb = keep.tile([P, NB, H], F32, name="out_sb")
         ident = keep.tile([P, P], F32, name="ident")
-        bsum = keep.tile([P, P], F32, name="bsum")
-        bih = keep.tile([32, P], BF16, name="bih")
-        bhh = keep.tile([32, P], BF16, name="bhh")
+        bsum = keep.tile([P, 2 * P], F32, name="bsum")
+        bih = keep.tile([16, 2 * P], BF16, name="bih")
+        bhh = keep.tile([16, 2 * P], BF16, name="bhh")
         bias_sb = keep.tile([P, 32], F32, name="bias_sb")
+        bsum_block = keep.tile([P, 2 * P], F32, name="bsum_block")
+        bias_block = keep.tile([P, 32], F32, name="bias_block")
         warm_in = keep.tile([P, 1], F32, name="warm_in")
         warm_out = keep.tile([P, 1], F32, name="warm_out")
 
-        x_view = x.rearrange("(p t) k -> p (t k)", t=NB)
-        out_view = out.rearrange("(p t) h -> p t h", t=NB)
+        x_view = x.rearrange("(t p) k -> p t k", p=P)
+        out_view = out.rearrange("(t p) h -> p t h", p=P)
         x_words = x_sb[:].bitcast(F32)
         w_words = w_sb[:].bitcast(F32)
 
@@ -62,7 +66,9 @@ def tile_lstmbaseline_pa_kernel(tc, x, W_ih0, b_ih0, b_hh0, out):
 
         def load_x(pair):
             cols = slice(pair * 2 * D, (pair + 1) * 2 * D)
-            nc.sync.dma_start(out=x_sb[:, cols], in_=x_view[:, cols])
+            nc.sync.dma_start(
+                out=x_sb[:, cols].rearrange("p (t k) -> p t k", t=2), in_=x_view[:, 2 * pair : 2 * pair + 2, :]
+            )
 
         def load_w(gi, ht, count):
             slot = gi * NH + ht
@@ -87,10 +93,15 @@ def tile_lstmbaseline_pa_kernel(tc, x, W_ih0, b_ih0, b_hh0, out):
                     nc.tensor.transpose(ps[:, u * 256 + r * P : u * 256 + (r + 1) * P], src, ident[:])
             return ps
 
-        def prep_copy(engine, ps):
+        def prep_copy(engine, ps, job=None):
             grouped = work.tile([P, 1024], BF16, name="grouped", tag="grouped", bufs=4, align_bytes=64)
-            dst = grouped[:].bitcast(F32).rearrange("p (c u) -> p c u", u=2)
-            src = ps[:].rearrange("p (u c) -> p c u", u=2)
+            dst = grouped[:].bitcast(F32)
+            if job is not None and job[0] == "w" and job[2] in BLOCK_HP:
+                dst = dst.rearrange("p (t q r u) -> p t q r u", t=2, q=4, u=2)
+                src = ps[:].rearrange("p (u q t r) -> p t q r u", u=2, q=4, t=2)
+            else:
+                dst = dst.rearrange("p (c u) -> p c u", u=2)
+                src = ps[:].rearrange("p (u c) -> p c u", u=2)
             if engine == "v":
                 nc.vector.tensor_copy(out=dst, in_=src)
             else:
@@ -140,12 +151,13 @@ def tile_lstmbaseline_pa_kernel(tc, x, W_ih0, b_ih0, b_hh0, out):
             ht, grp = units[n]
             if (n, gi) not in acts:
                 acts[(n, gi)] = work.tile([P, 512], F32, name="gate%d" % gi, tag="gate%d" % gi, bufs=4)
-            col = GATE_ROW_TILE[gi] + ht
+            bias = bias_block if ht // 2 in BLOCK_HP else bias_sb
+            col = 16 * (ht % 2) + (GATE_ROW_TILE[gi] + ht) // 2
             nc.scalar.activation(
                 out=acts[(n, gi)][:, c0:c1],
                 in_=ps[:, first : first + c1 - c0],
                 func=AF.Tanh if gi == 1 else AF.Sigmoid,
-                bias=bias_sb[:, col : col + 1],
+                bias=bias[:, col : col + 1],
                 scale=1.0,
             )
 
@@ -163,6 +175,34 @@ def tile_lstmbaseline_pa_kernel(tc, x, W_ih0, b_ih0, b_hh0, out):
                 )
             return ps
 
+        pair_t = {}
+
+        def block_product(n):
+            j, t = n // 2, n % 2
+            if t == 0:
+                pair_t[j] = work.tile([P, 1024], F32, name="prod", tag="prod", bufs=2, align_bytes=64)
+            nc.vector.tensor_tensor(
+                out=pair_t[j][:].rearrange("p (b t r) -> p b t r", t=2, r=32)[:, :, t, :],
+                in0=acts[(n, 2)][:].rearrange("p (b r) -> p b r", r=32),
+                in1=th[n][:].rearrange("p (b r) -> p b r", r=32),
+                op=ALU.mult,
+            )
+
+        def block_turn(j):
+            ht, grp = units[2 * j]
+            turned = work.tile([P, 1024], F32, name="turned", tag="turned", bufs=2, align_bytes=64)
+            nc.vector.transpose(turned[:], pair_t[j][:])
+            for q in range(4):
+                h0 = ht * P + 64 * q
+                nc.sync.dma_start(
+                    out=out[512 * grp : 512 * grp + 512, h0 : h0 + 64].rearrange("(b r) h -> r b h", r=32),
+                    in_=turned[32 * q : 32 * q + 32, :].rearrange("p (b h) -> p b h", h=64),
+                )
+
+        def act_c_block(n):
+            th[n] = work.tile([P, 512], F32, name="th", tag="th")
+            nc.scalar.activation(out=th[n][:], in_=c_t[n][:], func=AF.Tanh)
+
         def act_c(n, ps, c0, c1, first=0):
             if n not in th:
                 th[n] = work.tile([P, 512], F32, name="th", tag="th")
@@ -171,18 +211,28 @@ def tile_lstmbaseline_pa_kernel(tc, x, W_ih0, b_ih0, b_hh0, out):
         def final(n, t0, t1, ps=None, first=0):
             ht, grp = units[n]
             ps = o_ps[n] if ps is None else ps
+            dst = out_sb[:, 4 * grp + t0 : 4 * grp + t1, :]
+            split = "p (t m) -> p t m"
+            dims = {"m": P}
+            if ht // 2 in BLOCK_HP:
+                h0 = (ht // 2) * 2 * P
+                dst = dst[:, :, h0 : h0 + 2 * P].rearrange("p b (q t r) -> p b q t r", q=4, t=2)[:, :, :, ht % 2, :]
+                split = "p (b q r) -> p b q r"
+                dims = {"q": 4, "r": 32}
+            else:
+                dst = dst[:, :, ht * P : (ht + 1) * P]
             nc.vector.tensor_tensor(
-                out=out_sb[:, 4 * grp + t0 : 4 * grp + t1, ht * P : (ht + 1) * P],
-                in0=ps[:, (t0 - first) * P : (t1 - first) * P].rearrange("p (t m) -> p t m", m=P),
-                in1=th[n][:, t0 * P : t1 * P].rearrange("p (t m) -> p t m", m=P),
+                out=dst,
+                in0=ps[:, (t0 - first) * P : (t1 - first) * P].rearrange(split, **dims),
+                in1=th[n][:, t0 * P : t1 * P].rearrange(split, **dims),
                 op=ALU.mult,
             )
 
         def store(t0, t1, h0, h1):
             nc.sync.dma_start(out=out_view[:, t0:t1, h0:h1], in_=out_sb[:, t0:t1, h0:h1])
 
-        nc.scalar.dma_start(out=bih[:], in_=b_ih0.rearrange("(t p) -> t p", p=P))
-        nc.scalar.dma_start(out=bhh[:], in_=b_hh0.rearrange("(t p) -> t p", p=P))
+        nc.scalar.dma_start(out=bih[:], in_=b_ih0.rearrange("(g m) -> g m", m=2 * P))
+        nc.scalar.dma_start(out=bhh[:], in_=b_hh0.rearrange("(g m) -> g m", m=2 * P))
         load_w(0, 0, 1)
         load_w(0, 1, 1)
         load_x(0)
@@ -198,7 +248,8 @@ def tile_lstmbaseline_pa_kernel(tc, x, W_ih0, b_ih0, b_hh0, out):
         zeros = keep.tile([P, 512], BF16, name="zeros")
         nc.vector.memset(zeros[:], 0.0)
         nc.vector.memset(warm_in[:], 0.0)
-        nc.vector.memset(bsum[:], 0.0)
+        nc.vector.memset(bsum_block[:], 0.0)
+        nc.gpsimd.memset(bsum[:], 0.0)
         make_identity(nc, ident[:])
         nc.scalar.activation(out=warm_out[:], in_=warm_in[:], func=AF.Sigmoid)
         ps_warm = bank("m3")
@@ -213,79 +264,114 @@ def tile_lstmbaseline_pa_kernel(tc, x, W_ih0, b_ih0, b_hh0, out):
         j_v = [("w", gi, 1) for gi in range(3)]
         j_x = [("x", k, 0) for k in range(4)]
         p_wi = prep_transpose(j_w[0], "o1")
-        nc.vector.tensor_tensor(out=bsum[0:32, :], in0=bih[:], in1=bhh[:], op=ALU.add)
+        dealt = "g (q t r) -> g t q r"
+        nc.vector.tensor_tensor(
+            out=bsum_block[0:16, :].rearrange("g (t q r) -> g t q r", t=2, q=4),
+            in0=bih[:].rearrange(dealt, q=4, t=2),
+            in1=bhh[:].rearrange(dealt, q=4, t=2),
+            op=ALU.add,
+        )
         p_b = bank("c0")
-        nc.tensor.transpose(p_b[:, 0:P], bsum[:], ident[:])
+        for t in range(2):
+            nc.tensor.transpose(p_b[:, t * P : (t + 1) * P], bsum_block[:, t * P : (t + 1) * P], ident[:])
         p_x0 = prep_transpose(j_x[0], "in0")
         dummy(1)
         p_x1 = prep_transpose(j_x[1], "o0")
         dummy(1)
-        g_wi = prep_copy("v", p_wi)
-        nc.vector.tensor_copy(out=bias_sb[:], in_=p_b[:, 0:32])
+        g_wi = prep_copy("v", p_wi, j_w[0])
+        nc.vector.tensor_copy(
+            out=bias_block[:].rearrange("p (t g) -> p t g", t=2),
+            in_=p_b[:, 0 : 2 * P].rearrange("p (t m) -> p t m", t=2)[:, :, 0:16],
+        )
         g_x0 = prep_copy("s", p_x0)
         prep_quant(j_w[0], g_wi)
         g_x1 = prep_copy("s", p_x1)
         prep_quant(j_x[0], g_x0)
         p_wg = prep_transpose(j_w[1], "o1")
-        g_wg = prep_copy("s", p_wg)
+        g_wg = prep_copy("s", p_wg, j_w[1])
         p_wo = prep_transpose(j_w[2], "in0")
-        ia = [mx_pass(0, 0, 0, 256), mx_pass(1, 0, 0, 256)]
         prep_quant(j_x[1], g_x1)
-        g_wo = prep_copy("v", p_wo)
+        g_wo = prep_copy("v", p_wo, j_w[2])
+        ia = [mx_pass(0, 0, 0, 256), mx_pass(1, 0, 0, 256)]
         ib = [mx_pass(0, 0, 256, 512), mx_pass(1, 0, 256, 512)]
         act_gate(0, 0, ia[0], 0, 256)
         act_gate(1, 0, ia[1], 0, 256)
         act_gate(0, 0, ib[0], 256, 512)
         act_gate(1, 0, ib[1], 256, 512)
-        p_x2 = prep_transpose(j_x[2], "o0")
         prep_quant(j_w[1], g_wg)
-        g_x2 = prep_copy("v", p_x2)
         prep_quant(j_w[2], g_wo)
+        p_x2 = prep_transpose(j_x[2], "c0")
+        p_x3 = prep_transpose(j_x[3], "o0")
+        g_x2 = prep_copy("v", p_x2)
+        g_x3 = prep_copy("v", p_x3)
         gg = [mx_pass(0, 1, 0, 512), mx_pass(1, 1, 0, 512)]
-        p_x3 = prep_transpose(j_x[3], "c0")
         act_gate(0, 1, gg[0], 0, 512)
         act_gate(1, 1, gg[1], 0, 512)
         cmult(nc.gpsimd, 0, 0, 512)
-        cmult(nc.gpsimd, 1, 0, 512)
-        g_x3 = prep_copy("v", p_x3)
-        prep_quant(j_x[2], g_x2)
         oo = [mx_pass(0, 2, 0, 512), mx_pass(1, 2, 0, 512)]
+        prep_quant(j_x[2], g_x2)
         prep_quant(j_x[3], g_x3)
         p_v = prep_transpose(j_v[0], "o1")
-        g_v = prep_copy("v", p_v)
+        g_v = prep_copy("v", p_v, j_v[0])
+        cmult(nc.vector, 1, 0, 512)
         act_gate(0, 2, oo[0], 0, 512)
         act_gate(1, 2, oo[1], 0, 512)
         nxt = [mx_pass(2, gi, 0, 512) for gi in range(3)]
         pending = [(j_v[0], g_v)]
+
+        nc.vector.tensor_tensor(out=bsum[0:16, :], in0=bih[:], in1=bhh[:], op=ALU.add)
 
         jobs = {2: [(j_v[1], "in0"), (j_v[2], "o1")]}
         for hp in (2, 3):
             for gi in range(3):
                 jobs[4 * hp - 4 + gi] = [(("w", gi, hp), "in0")]
 
+        def finish(m):
+            j = m // 2
+            ht, grp = units[m]
+            if j in BLOCK_PAIRS:
+                block_product(m)
+            else:
+                final(m, 0, 4)
+                if m % 2 == 1:
+                    store(4 * grp, 4 * grp + 4, (ht - 1) * P, (ht + 1) * P)
+
         for n in range(2, NU - 2):
             k = n - 2
+            if n > 3:
+                finish(k - 1)
+            elif n == 3:
+                finish(0)
             if n > 2:
                 for job, grouped in pending:
                     prep_quant(job, grouped)
                 pending = []
-                if k > 0:
-                    final(k - 1, 0, 4)
-                    ht, grp = units[k - 1]
-                    if ht % 2 == 1:
-                        store(4 * grp, 4 * grp + 4, (ht - 1) * P, (ht + 1) * P)
-            o_ps[k] = back_transpose(acts[(k, 2)], bank("o%d" % (k % 2)), 0, 4)
-            c_ps[k] = back_transpose(c_t[k], bank("c0"), 0, 4)
+            if n > 3 and k % 2 == 0 and (k - 1) // 2 in BLOCK_PAIRS:
+                block_turn((k - 1) // 2)
+            if k // 2 not in BLOCK_PAIRS:
+                o_ps[k] = back_transpose(acts[(k, 2)], bank("o%d" % (k % 2)), 0, 4)
+                c_ps[k] = back_transpose(c_t[k], bank("c0"), 0, 4)
             banks = [(job, prep_transpose(job, tag)) for job, tag in jobs.get(n, [])]
+            if n == 3:
+                p_b = bank("in0")
+                for t in range(2):
+                    nc.tensor.transpose(p_b[:, t * P : (t + 1) * P], bsum[:, t * P : (t + 1) * P], ident[:])
+                nc.vector.tensor_copy(
+                    out=bias_sb[:].rearrange("p (t g) -> p t g", t=2),
+                    in_=p_b[:, 0 : 2 * P].rearrange("p (t m) -> p t m", t=2)[:, :, 0:16],
+                )
             cur = nxt
             act_gate(n, 0, cur[0], 0, 512)
             act_gate(n, 1, cur[1], 0, 512)
             nxt = [mx_pass(n + 1, gi, 0, 512) for gi in range(3)]
             act_gate(n, 2, cur[2], 0, 512)
-            act_c(k, c_ps[k], 0, 512)
+            if k // 2 in BLOCK_PAIRS:
+                act_c_block(k)
+            else:
+                act_c(k, c_ps[k], 0, 512)
             cmult(nc.gpsimd, n, 0, 512)
             for job, ps in banks:
-                grouped = prep_copy("v", ps)
+                grouped = prep_copy("v", ps, job)
                 if n == 2:
                     prep_quant(*pending.pop(0))
                 pending.append((job, grouped))
@@ -296,9 +382,9 @@ def tile_lstmbaseline_pa_kernel(tc, x, W_ih0, b_ih0, b_hh0, out):
             ht, grp = units[n]
             store(4 * grp + t0, 4 * grp + t1, ht * P, (ht + 1) * P)
 
-        final(a - 3, 0, 4)
-        ht, grp = units[a - 3]
-        store(4 * grp, 4 * grp + 4, (ht - 1) * P, (ht + 1) * P)
+        finish(a - 3)
+        if (a - 3) // 2 in BLOCK_PAIRS:
+            block_turn((a - 3) // 2)
         o_ps[a - 2] = back_transpose(acts[(a - 2, 2)], bank("o%d" % ((a - 2) % 2)), 0, 4)
         c_ps[a - 2] = back_transpose(c_t[a - 2], bank("c0"), 0, 4)
         act_gate(a, 0, nxt[0], 0, 512)

@@ -19,8 +19,8 @@ BYTES = B * D * 2 + 3 * H * D * 2 + 2 * 3 * H * 2 + B * H * 4
 NB = B // P
 NH = H // P
 GATE_ROW_TILE = (0, 16, 24)
-BLOCK_HP = (0, 1, 2)
-BLOCK_PAIRS = (0, 1, 2, 3, 4, 5)
+BLOCK_HP = (0, 1)
+BLOCK_PAIRS = (1, 3)
 WARM = 5
 
 
@@ -369,7 +369,7 @@ def tile_lstmbaseline_pa_kernel(tc, x, W_ih0, b_ih0, b_hh0, out):
                 act_c_block(k)
             else:
                 act_c(k, c_ps[k], 0, 512)
-            cmult(nc.gpsimd, n, 0, 512)
+            cmult(nc.gpsimd if n % 2 == 0 or n // 2 in BLOCK_PAIRS else nc.vector, n, 0, 512)
             for job, ps in banks:
                 grouped = prep_copy("v", ps, job)
                 if n == 2:

@@ -19,8 +19,8 @@ BYTES = B * D * 2 + 3 * H * D * 2 + 2 * 3 * H * 2 + B * H * 4
 NB = B // P
 NH = H // P
 GATE_ROW_TILE = (0, 16, 24)
-BLOCK_HP = (0, 1)
-BLOCK_PAIRS = (1, 3)
+BLOCK_HP = (0, 1, 2,)
+BLOCK_PAIRS = (0, 2, 4,)
 WARM = 5
 
 
@@ -272,21 +272,29 @@ def tile_lstmbaseline_pa_kernel(tc, x, W_ih0, b_ih0, b_hh0, out):
             op=ALU.add,
         )
         p_b = bank("c0")
-        for t in range(2):
-            nc.tensor.transpose(p_b[:, t * P : (t + 1) * P], bsum_block[:, t * P : (t + 1) * P], ident[:])
+
+        def turn_bias(t):
+            nc.tensor.matmul(
+                out=p_b[:, t * P : (t + 1) * P],
+                lhsT=bsum_block[:, t * P : (t + 1) * P],
+                rhs=ident[:],
+                start=True,
+                stop=True,
+            )
+
+        turn_bias(0)
         p_x0 = prep_transpose(j_x[0], "in0")
-        dummy(1)
         p_x1 = prep_transpose(j_x[1], "o0")
-        dummy(1)
+        turn_bias(1)
         g_wi = prep_copy("v", p_wi, j_w[0])
-        nc.vector.tensor_copy(
-            out=bias_block[:].rearrange("p (t g) -> p t g", t=2),
-            in_=p_b[:, 0 : 2 * P].rearrange("p (t m) -> p t m", t=2)[:, :, 0:16],
-        )
         g_x0 = prep_copy("s", p_x0)
         prep_quant(j_w[0], g_wi)
         g_x1 = prep_copy("s", p_x1)
         prep_quant(j_x[0], g_x0)
+        nc.vector.tensor_copy(
+            out=bias_block[:].rearrange("p (t g) -> p t g", t=2),
+            in_=p_b[:, 0 : 2 * P].rearrange("p (t m) -> p t m", t=2)[:, :, 0:16],
+        )
         p_wg = prep_transpose(j_w[1], "o1")
         g_wg = prep_copy("s", p_wg, j_w[1])
         p_wo = prep_transpose(j_w[2], "in0")
@@ -322,9 +330,9 @@ def tile_lstmbaseline_pa_kernel(tc, x, W_ih0, b_ih0, b_hh0, out):
         nc.vector.tensor_tensor(out=bsum[0:16, :], in0=bih[:], in1=bhh[:], op=ALU.add)
 
         jobs = {2: [(j_v[1], "in0"), (j_v[2], "o1")]}
-        for hp in (2, 3):
-            for gi in range(3):
-                jobs[4 * hp - 4 + gi] = [(("w", gi, hp), "in0")]
+        later = [("w", gi, hp) for hp in (2, 3) for gi in range(3)]
+        for n, count in {5:1,6:2,9:1,10:2}.items():
+            jobs[n] = [(later.pop(0), tag) for tag in ("in0", "c0")[:count]]
 
         def finish(m):
             j = m // 2

@@ -125,6 +125,9 @@ def tile_lstmbaseline_pa_kernel(tc, x, W_ih0, b_ih0, b_hh0, out):
                     units.append((ht, grp))
         NU = len(units)
         acts = {}
+        pair_o = {}
+        pair_c = {}
+        pair_th = {}
         c_t = {}
         c_ps = {}
         o_ps = {}
@@ -150,7 +153,13 @@ def tile_lstmbaseline_pa_kernel(tc, x, W_ih0, b_ih0, b_hh0, out):
             first = 0 if first is None else first
             ht, grp = units[n]
             if (n, gi) not in acts:
-                acts[(n, gi)] = work.tile([P, 512], F32, name="gate%d" % gi, tag="gate%d" % gi, bufs=4)
+                if gi == 2 and n // 2 in BLOCK_PAIRS:
+                    both = work.tile([P, 1024], F32, name="o_pair", tag="o_pair", bufs=2)
+                    pair_o[n // 2] = both
+                    for t in range(2):
+                        acts[(n // 2 * 2 + t, 2)] = both[:, t * 512 : (t + 1) * 512]
+                else:
+                    acts[(n, gi)] = work.tile([P, 512], F32, name="gate%d" % gi, tag="gate%d" % gi, bufs=4)
             bias = bias_block if ht // 2 in BLOCK_HP else bias_sb
             col = 16 * (ht % 2) + (GATE_ROW_TILE[gi] + ht) // 2
             nc.scalar.activation(
@@ -163,7 +172,13 @@ def tile_lstmbaseline_pa_kernel(tc, x, W_ih0, b_ih0, b_hh0, out):
 
         def cmult(engine, n, c0, c1):
             if n not in c_t:
-                c_t[n] = work.tile([P, 512], F32, name="c_t", tag="c_t", bufs=4)
+                if n // 2 in BLOCK_PAIRS:
+                    both = work.tile([P, 1024], F32, name="c_pair", tag="c_pair", bufs=2)
+                    pair_c[n // 2] = both
+                    for t in range(2):
+                        c_t[n // 2 * 2 + t] = both[:, t * 512 : (t + 1) * 512]
+                else:
+                    c_t[n] = work.tile([P, 512], F32, name="c_t", tag="c_t", bufs=4)
             engine.tensor_tensor(
                 out=c_t[n][:, c0:c1], in0=acts[(n, 0)][:, c0:c1], in1=acts[(n, 1)][:, c0:c1], op=ALU.mult
             )
@@ -175,33 +190,31 @@ def tile_lstmbaseline_pa_kernel(tc, x, W_ih0, b_ih0, b_hh0, out):
                 )
             return ps
 
-        pair_t = {}
+        def act_c_block(j):
+            pair_th[j] = work.tile([P, 1024], F32, name="th_pair", tag="th_pair", bufs=2)
+            nc.scalar.activation(out=pair_th[j][:], in_=pair_c[j][:], func=AF.Tanh)
 
-        def block_product(n):
-            j, t = n // 2, n % 2
-            if t == 0:
-                pair_t[j] = work.tile([P, 1024], F32, name="prod", tag="prod", bufs=2, align_bytes=64)
+        def block_finish(j):
+            ht, grp = units[2 * j]
+            prod = work.tile([P, 1024], F32, name="prod", tag="prod", bufs=2, align_bytes=64)
             nc.vector.tensor_tensor(
-                out=pair_t[j][:].rearrange("p (b t r) -> p b t r", t=2, r=32)[:, :, t, :],
-                in0=acts[(n, 2)][:].rearrange("p (b r) -> p b r", r=32),
-                in1=th[n][:].rearrange("p (b r) -> p b r", r=32),
+                out=prod[:].rearrange("p (b t r) -> p b t r", t=2, r=32),
+                in0=pair_o[j][:].rearrange("p (t b r) -> p b t r", t=2, r=32),
+                in1=pair_th[j][:].rearrange("p (t b r) -> p b t r", t=2, r=32),
                 op=ALU.mult,
             )
+            return prod
 
-        def block_turn(j):
+        def block_turn(j, prod):
             ht, grp = units[2 * j]
             turned = work.tile([P, 1024], F32, name="turned", tag="turned", bufs=2, align_bytes=64)
-            nc.vector.transpose(turned[:], pair_t[j][:])
+            nc.vector.transpose(turned[:], prod[:])
             for q in range(4):
                 h0 = ht * P + 64 * q
                 nc.sync.dma_start(
                     out=out[512 * grp : 512 * grp + 512, h0 : h0 + 64].rearrange("(b r) h -> r b h", r=32),
                     in_=turned[32 * q : 32 * q + 32, :].rearrange("p (b h) -> p b h", h=64),
                 )
-
-        def act_c_block(n):
-            th[n] = work.tile([P, 512], F32, name="th", tag="th")
-            nc.scalar.activation(out=th[n][:], in_=c_t[n][:], func=AF.Tanh)
 
         def act_c(n, ps, c0, c1, first=0):
             if n not in th:
@@ -335,28 +348,24 @@ def tile_lstmbaseline_pa_kernel(tc, x, W_ih0, b_ih0, b_hh0, out):
             jobs[n] = [(later.pop(0), tag) for tag in ("in0", "c0")[:count]]
 
         def finish(m):
-            j = m // 2
             ht, grp = units[m]
-            if j in BLOCK_PAIRS:
-                block_product(m)
-            else:
-                final(m, 0, 4)
-                if m % 2 == 1:
-                    store(4 * grp, 4 * grp + 4, (ht - 1) * P, (ht + 1) * P)
+            final(m, 0, 4)
+            if m % 2 == 1:
+                store(4 * grp, 4 * grp + 4, (ht - 1) * P, (ht + 1) * P)
 
         for n in range(2, NU - 2):
             k = n - 2
-            if n > 3:
+            block = k // 2 in BLOCK_PAIRS
+            prod = None
+            if k > 0 and (k - 1) // 2 not in BLOCK_PAIRS:
                 finish(k - 1)
-            elif n == 3:
-                finish(0)
             if n > 2:
                 for job, grouped in pending:
                     prep_quant(job, grouped)
                 pending = []
-            if n > 3 and k % 2 == 0 and (k - 1) // 2 in BLOCK_PAIRS:
-                block_turn((k - 1) // 2)
-            if k // 2 not in BLOCK_PAIRS:
+            if block and k % 2 == 1:
+                prod = block_finish(k // 2)
+            if not block:
                 o_ps[k] = back_transpose(acts[(k, 2)], bank("o%d" % (k % 2)), 0, 4)
                 c_ps[k] = back_transpose(c_t[k], bank("c0"), 0, 4)
             banks = [(job, prep_transpose(job, tag)) for job, tag in jobs.get(n, [])]
@@ -373,11 +382,13 @@ def tile_lstmbaseline_pa_kernel(tc, x, W_ih0, b_ih0, b_hh0, out):
             act_gate(n, 1, cur[1], 0, 512)
             nxt = [mx_pass(n + 1, gi, 0, 512) for gi in range(3)]
             act_gate(n, 2, cur[2], 0, 512)
-            if k // 2 in BLOCK_PAIRS:
-                act_c_block(k)
-            else:
+            if not block:
                 act_c(k, c_ps[k], 0, 512)
+            elif k % 2 == 0:
+                act_c_block(k // 2)
             cmult(nc.gpsimd if n % 2 == 0 or n // 2 in BLOCK_PAIRS else nc.vector, n, 0, 512)
+            if prod is not None:
+                block_turn(k // 2, prod)
             for job, ps in banks:
                 grouped = prep_copy("v", ps, job)
                 if n == 2:
@@ -391,8 +402,6 @@ def tile_lstmbaseline_pa_kernel(tc, x, W_ih0, b_ih0, b_hh0, out):
             store(4 * grp + t0, 4 * grp + t1, ht * P, (ht + 1) * P)
 
         finish(a - 3)
-        if (a - 3) // 2 in BLOCK_PAIRS:
-            block_turn((a - 3) // 2)
         o_ps[a - 2] = back_transpose(acts[(a - 2, 2)], bank("o%d" % ((a - 2) % 2)), 0, 4)
         c_ps[a - 2] = back_transpose(c_t[a - 2], bank("c0"), 0, 4)
         act_gate(a, 0, nxt[0], 0, 512)

from contextlib import ExitStack

import concourse.mybir as mybir
from concourse.masks import make_identity

F32 = mybir.dt.float32
BF16 = mybir.dt.bfloat16
U32 = mybir.dt.uint32
U8 = mybir.dt.uint8
FP8X4 = mybir.dt.float8_e4m3fn_x4
AF = mybir.ActivationFunctionType
ALU = mybir.AluOpType

P = 128
B, D, H = 1024, 512, 1024
FLOPS = 2 * B * D * 3 * H
BYTES = B * D * 2 + 3 * H * D * 2 + 2 * 3 * H * 2 + B * H * 4

NB = B // P
NH = H // P
GATE_ROW_TILE = (0, 16, 24)
BLOCK_HP = (0, 1, 2,)
BLOCK_PAIRS = (0, 2, 4,)
WARM = 5


def tile_lstmbaseline_pa_kernel(tc, x, W_ih0, b_ih0, b_hh0, out):
    nc = tc.nc
    with ExitStack() as ctx:
        keep = ctx.enter_context(tc.tile_pool(name="keep", bufs=1))
        work = ctx.enter_context(tc.tile_pool(name="work", bufs=3))
        psum = ctx.enter_context(tc.psum_pool(name="psum", bufs=1))
        ctx.enter_context(tc.manual_schedule())

        x_sb = keep.tile([P, NB * D], BF16, name="x_sb")
        w_sb = keep.tile([P, 3 * NH * D], BF16, name="w_sb")
        xq = keep.tile([P, B], U32, name="xq", align_bytes=64)
        xs = keep.tile([P, B], U8, name="xs", align_bytes=64)
        wq = keep.tile([P, 3 * H], U32, name="wq", align_bytes=64)
        ws = keep.tile([P, 3 * H], U8, name="ws", align_bytes=64)
        out_sb = keep.tile([P, NB, H], F32, name="out_sb")
        ident = keep.tile([P, P], F32, name="ident")
        bsum = keep.tile([P, 2 * P], F32, name="bsum")
        bih = keep.tile([16, 2 * P], BF16, name="bih")
        bhh = keep.tile([16, 2 * P], BF16, name="bhh")
        bias_sb = keep.tile([P, 32], F32, name="bias_sb")
        bsum_block = keep.tile([P, 2 * P], F32, name="bsum_block")
        bias_block = keep.tile([P, 32], F32, name="bias_block")
        warm_in = keep.tile([P, 1], F32, name="warm_in")
        warm_out = keep.tile([P, 1], F32, name="warm_out")

        x_view = x.rearrange("(t p) k -> p t k", p=P)
        out_view = out.rearrange("(t p) h -> p t h", p=P)
        x_words = x_sb[:].bitcast(F32)
        w_words = w_sb[:].bitcast(F32)

        def bank(tag):
            return psum.tile([P, 512], F32, name="ps_" + tag, tag=tag)

        mx_count = [0]

        def mx_bank():
            tag = "m%d" % (mx_count[0] % 4)
            mx_count[0] += 1
            return bank(tag)

        def load_x(pair):
            cols = slice(pair * 2 * D, (pair + 1) * 2 * D)
            nc.sync.dma_start(
                out=x_sb[:, cols].rearrange("p (t k) -> p t k", t=2), in_=x_view[:, 2 * pair : 2 * pair + 2, :]
            )

        def load_w(gi, ht, count):
            slot = gi * NH + ht
            row = (GATE_ROW_TILE[gi] + ht) * P
            nc.sync.dma_start(
                out=w_sb[:, slot * D : (slot + count) * D].rearrange("p (t k) -> p t k", t=count),
                in_=W_ih0[row : row + count * P, :].rearrange("(t p) k -> p t k", p=P),
            )

        def job_words(job):
            kind, a, b2 = job
            if kind == "x":
                return x_words, a * 2
            return w_words, a * NH + 2 * b2

        def prep_transpose(job, tag):
            words, first = job_words(job)
            ps = bank(tag)
            for r in range(2):
                for u in range(2):
                    src = words[:, (first + r) * 256 + u : (first + r + 1) * 256 : 2]
                    nc.tensor.transpose(ps[:, u * 256 + r * P : u * 256 + (r + 1) * P], src, ident[:])
            return ps

        def prep_copy(engine, ps, job=None):
            grouped = work.tile([P, 1024], BF16, name="grouped", tag="grouped", bufs=4, align_bytes=64)
            dst = grouped[:].bitcast(F32)
            if job is not None and job[0] == "w" and job[2] in BLOCK_HP:
                dst = dst.rearrange("p (t q r u) -> p t q r u", t=2, q=4, u=2)
                src = ps[:].rearrange("p (u q t r) -> p t q r u", u=2, q=4, t=2)
            else:
                dst = dst.rearrange("p (c u) -> p c u", u=2)
                src = ps[:].rearrange("p (u c) -> p c u", u=2)
            if engine == "v":
                nc.vector.tensor_copy(out=dst, in_=src)
            else:
                nc.scalar.copy(out=dst, in_=src)
            return grouped

        def prep_quant(job, grouped):
            kind, a, b2 = job
            if kind == "x":
                codes, scales, c0 = xq, xs, a * 256
            else:
                codes, scales, c0 = wq, ws, (a * NH + 2 * b2) * P
            nc.vector.quantize_mx(
                out=codes[:, c0 : c0 + 256].bitcast(FP8X4), scales=scales[:, c0 : c0 + 256], in_=grouped[:]
            )

        units = []
        for hp in range(NH // 2):
            for grp in range(2):
                for ht in (2 * hp, 2 * hp + 1):
                    units.append((ht, grp))
        NU = len(units)
        acts = {}
        pair_o = {}
        pair_c = {}
        pair_th = {}
        c_t = {}
        c_ps = {}
        o_ps = {}
        th = {}

        def mx_pass(n, gi, c0, c1, ps=None):
            ht, grp = units[n]
            ps = mx_bank() if ps is None else ps
            slot = gi * NH + ht
            cols = slice(grp * 512 + c0, grp * 512 + c1)
            nc.tensor.matmul_mx(
                out=ps[:, 0 : c1 - c0],
                lhsT=wq[:, slot * P : (slot + 1) * P].bitcast(FP8X4),
                lhsT_scale=ws[:, slot * P : (slot + 1) * P],
                rhs=xq[:, cols].bitcast(FP8X4),
                rhs_scale=xs[:, cols],
                start=True,
                stop=True,
            )
            return ps

        def act_gate(n, gi, ps, c0, c1, first=None):
            first = 0 if first is None else first
            ht, grp = units[n]
            if (n, gi) not in acts:
                if gi == 2 and n // 2 in BLOCK_PAIRS:
                    both = work.tile([P, 1024], F32, name="o_pair", tag="o_pair", bufs=2)
                    pair_o[n // 2] = both
                    for t in range(2):
                        acts[(n // 2 * 2 + t, 2)] = both[:, t * 512 : (t + 1) * 512]
                else:
                    acts[(n, gi)] = work.tile([P, 512], F32, name="gate%d" % gi, tag="gate%d" % gi, bufs=4)
            bias = bias_block if ht // 2 in BLOCK_HP else bias_sb
            col = 16 * (ht % 2) + (GATE_ROW_TILE[gi] + ht) // 2
            nc.scalar.activation(
                out=acts[(n, gi)][:, c0:c1],
                in_=ps[:, first : first + c1 - c0],
                func=AF.Tanh if gi == 1 else AF.Sigmoid,
                bias=bias[:, col : col + 1],
                scale=1.0,
            )

        def cmult(engine, n, c0, c1):
            if n not in c_t:
                if n // 2 in BLOCK_PAIRS:
                    both = work.tile([P, 1024], F32, name="c_pair", tag="c_pair", bufs=2)
                    pair_c[n // 2] = both
                    for t in range(2):
                        c_t[n // 2 * 2 + t] = both[:, t * 512 : (t + 1) * 512]
                else:
                    c_t[n] = work.tile([P, 512], F32, name="c_t", tag="c_t", bufs=4)
            engine.tensor_tensor(
                out=c_t[n][:, c0:c1], in0=acts[(n, 0)][:, c0:c1], in1=acts[(n, 1)][:, c0:c1], op=ALU.mult
            )

        def back_transpose(src, ps, t0, t1):
            for tl in range(t0, t1):
                nc.tensor.transpose(
                    ps[:, (tl - t0) * P : (tl - t0 + 1) * P], src[:, tl * P : (tl + 1) * P], ident[:]
                )
            return ps

        def act_c_block(j):
            pair_th[j] = work.tile([P, 1024], F32, name="th_pair", tag="th_pair", bufs=2)
            nc.scalar.activation(out=pair_th[j][:], in_=pair_c[j][:], func=AF.Tanh)

        def block_finish(j):
            ht, grp = units[2 * j]
            prod = work.tile([P, 1024], F32, name="prod", tag="prod", bufs=2, align_bytes=64)
            nc.vector.tensor_tensor(
                out=prod[:].rearrange("p (b t r) -> p b t r", t=2, r=32),
                in0=pair_o[j][:].rearrange("p (t b r) -> p b t r", t=2, r=32),
                in1=pair_th[j][:].rearrange("p (t b r) -> p b t r", t=2, r=32),
                op=ALU.mult,
            )
            return prod

        def block_turn(j, prod):
            ht, grp = units[2 * j]
            turned = work.tile([P, 1024], F32, name="turned", tag="turned", bufs=2, align_bytes=64)
            nc.vector.transpose(turned[:], prod[:])
            for q in range(4):
                h0 = ht * P + 64 * q
                nc.sync.dma_start(
                    out=out[512 * grp : 512 * grp + 512, h0 : h0 + 64].rearrange("(b r) h -> r b h", r=32),
                    in_=turned[32 * q : 32 * q + 32, :].rearrange("p (b h) -> p b h", h=64),
                )

        def act_c(n, ps, c0, c1, first=0):
            if n not in th:
                th[n] = work.tile([P, 512], F32, name="th", tag="th")
            nc.scalar.activation(out=th[n][:, c0:c1], in_=ps[:, first : first + c1 - c0], func=AF.Tanh)

        def final(n, t0, t1, ps=None, first=0):
            ht, grp = units[n]
            ps = o_ps[n] if ps is None else ps
            dst = out_sb[:, 4 * grp + t0 : 4 * grp + t1, :]
            split = "p (t m) -> p t m"
            dims = {"m": P}
            if ht // 2 in BLOCK_HP:
                h0 = (ht // 2) * 2 * P
                dst = dst[:, :, h0 : h0 + 2 * P].rearrange("p b (q t r) -> p b q t r", q=4, t=2)[:, :, :, ht % 2, :]
                split = "p (b q r) -> p b q r"
                dims = {"q": 4, "r": 32}
            else:
                dst = dst[:, :, ht * P : (ht + 1) * P]
            nc.vector.tensor_tensor(
                out=dst,
                in0=ps[:, (t0 - first) * P : (t1 - first) * P].rearrange(split, **dims),
                in1=th[n][:, t0 * P : t1 * P].rearrange(split, **dims),
                op=ALU.mult,
            )

        def store(t0, t1, h0, h1):
            nc.sync.dma_start(out=out_view[:, t0:t1, h0:h1], in_=out_sb[:, t0:t1, h0:h1])

        nc.scalar.dma_start(out=bih[:], in_=b_ih0.rearrange("(g m) -> g m", m=2 * P))
        nc.scalar.dma_start(out=bhh[:], in_=b_hh0.rearrange("(g m) -> g m", m=2 * P))
        load_w(0, 0, 1)
        load_w(0, 1, 1)
        load_x(0)
        load_x(1)
        load_w(1, 0, 2)
        load_w(2, 0, 2)
        load_x(2)
        load_x(3)
        for hp in range(1, NH // 2):
            for gi in range(3):
                load_w(gi, 2 * hp, 2)

        zeros = keep.tile([P, 512], BF16, name="zeros")
        nc.vector.memset(zeros[:], 0.0)
        nc.vector.memset(warm_in[:], 0.0)
        nc.vector.memset(bsum_block[:], 0.0)
        nc.gpsimd.memset(bsum[:], 0.0)
        make_identity(nc, ident[:])
        nc.scalar.activation(out=warm_out[:], in_=warm_in[:], func=AF.Sigmoid)
        ps_warm = bank("m3")

        def dummy(count):
            for k in range(count):
                nc.tensor.matmul(out=ps_warm[:], lhsT=zeros[:, 0:P], rhs=zeros[:], start=True, stop=True)

        dummy(WARM)

        j_w = [("w", gi, 0) for gi in range(3)]
        j_v = [("w", gi, 1) for gi in range(3)]
        j_x = [("x", k, 0) for k in range(4)]
        p_wi = prep_transpose(j_w[0], "o1")
        dealt = "g (q t r) -> g t q r"
        nc.vector.tensor_tensor(
            out=bsum_block[0:16, :].rearrange("g (t q r) -> g t q r", t=2, q=4),
            in0=bih[:].rearrange(dealt, q=4, t=2),
            in1=bhh[:].rearrange(dealt, q=4, t=2),
            op=ALU.add,
        )
        p_b = bank("c0")

        def turn_bias(t):
            nc.tensor.matmul(
                out=p_b[:, t * P : (t + 1) * P],
                lhsT=bsum_block[:, t * P : (t + 1) * P],
                rhs=ident[:],
                start=True,
                stop=True,
            )

        turn_bias(0)
        p_x0 = prep_transpose(j_x[0], "in0")
        p_x1 = prep_transpose(j_x[1], "o0")
        turn_bias(1)
        g_wi = prep_copy("v", p_wi, j_w[0])
        g_x0 = prep_copy("s", p_x0)
        prep_quant(j_w[0], g_wi)
        g_x1 = prep_copy("s", p_x1)
        prep_quant(j_x[0], g_x0)
        nc.vector.tensor_copy(
            out=bias_block[:].rearrange("p (t g) -> p t g", t=2),
            in_=p_b[:, 0 : 2 * P].rearrange("p (t m) -> p t m", t=2)[:, :, 0:16],
        )
        p_wg = prep_transpose(j_w[1], "o1")
        g_wg = prep_copy("s", p_wg, j_w[1])
        p_wo = prep_transpose(j_w[2], "in0")
        prep_quant(j_x[1], g_x1)
        g_wo = prep_copy("v", p_wo, j_w[2])
        ia = [mx_pass(0, 0, 0, 256), mx_pass(1, 0, 0, 256)]
        ib = [mx_pass(0, 0, 256, 512), mx_pass(1, 0, 256, 512)]
        act_gate(0, 0, ia[0], 0, 256)
        act_gate(1, 0, ia[1], 0, 256)
        act_gate(0, 0, ib[0], 256, 512)
        act_gate(1, 0, ib[1], 256, 512)
        prep_quant(j_w[1], g_wg)
        prep_quant(j_w[2], g_wo)
        p_x2 = prep_transpose(j_x[2], "c0")
        p_x3 = prep_transpose(j_x[3], "o0")
        g_x2 = prep_copy("v", p_x2)
        g_x3 = prep_copy("v", p_x3)
        gg = [mx_pass(0, 1, 0, 512), mx_pass(1, 1, 0, 512)]
        act_gate(0, 1, gg[0], 0, 512)
        act_gate(1, 1, gg[1], 0, 512)
        cmult(nc.gpsimd, 0, 0, 512)
        oo = [mx_pass(0, 2, 0, 512), mx_pass(1, 2, 0, 512)]
        prep_quant(j_x[2], g_x2)
        prep_quant(j_x[3], g_x3)
        p_v = prep_transpose(j_v[0], "o1")
        g_v = prep_copy("v", p_v, j_v[0])
        cmult(nc.vector, 1, 0, 512)
        act_gate(0, 2, oo[0], 0, 512)
        act_gate(1, 2, oo[1], 0, 512)
        nxt = [mx_pass(2, gi, 0, 512) for gi in range(3)]
        pending = [(j_v[0], g_v)]

        nc.vector.tensor_tensor(out=bsum[0:16, :], in0=bih[:], in1=bhh[:], op=ALU.add)

        jobs = {2: [(j_v[1], "in0"), (j_v[2], "o1")]}
        later = [("w", gi, hp) for hp in (2, 3) for gi in range(3)]
        for n, count in {5:1,6:2,9:1,10:2}.items():
            jobs[n] = [(later.pop(0), tag) for tag in ("in0", "c0")[:count]]

        def finish(m):
            ht, grp = units[m]
            final(m, 0, 4)
            if m % 2 == 1:
                store(4 * grp, 4 * grp + 4, (ht - 1) * P, (ht + 1) * P)

        for n in range(2, NU - 2):
            k = n - 2
            block = k // 2 in BLOCK_PAIRS
            prod = None
            if k > 0 and (k - 1) // 2 not in BLOCK_PAIRS:
                finish(k - 1)
            if n > 2:
                for job, grouped in pending:
                    prep_quant(job, grouped)
                pending = []
            if block and k % 2 == 1:
                prod = block_finish(k // 2)
            if not block:
                o_ps[k] = back_transpose(acts[(k, 2)], bank("o%d" % (k % 2)), 0, 4)
                c_ps[k] = back_transpose(c_t[k], bank("c0"), 0, 4)
            banks = [(job, prep_transpose(job, tag)) for job, tag in jobs.get(n, [])]
            if n == 3:
                p_b = bank("in0")
                for t in range(2):
                    nc.tensor.transpose(p_b[:, t * P : (t + 1) * P], bsum[:, t * P : (t + 1) * P], ident[:])
                nc.vector.tensor_copy(
                    out=bias_sb[:].rearrange("p (t g) -> p t g", t=2),
                    in_=p_b[:, 0 : 2 * P].rearrange("p (t m) -> p t m", t=2)[:, :, 0:16],
                )
            cur = nxt
            act_gate(n, 0, cur[0], 0, 512)
            act_gate(n, 1, cur[1], 0, 512)
            nxt = [mx_pass(n + 1, gi, 0, 512) for gi in range(3)]
            act_gate(n, 2, cur[2], 0, 512)
            if not block:
                act_c(k, c_ps[k], 0, 512)
            elif k % 2 == 0:
                act_c_block(k // 2)
            cmult(nc.gpsimd if n % 2 == 0 or n // 2 in BLOCK_PAIRS else nc.vector, n, 0, 512)
            if prod is not None:
                block_turn(k // 2, prod)
            for job, ps in banks:
                grouped = prep_copy("v", ps, job)
                if n == 2:
                    prep_quant(*pending.pop(0))
                pending.append((job, grouped))

        a, z = NU - 2, NU - 1

        def store_unit(n, t0, t1):
            ht, grp = units[n]
            store(4 * grp + t0, 4 * grp + t1, ht * P, (ht + 1) * P)

        finish(a - 3)
        o_ps[a - 2] = back_transpose(acts[(a - 2, 2)], bank("o%d" % ((a - 2) % 2)), 0, 4)
        c_ps[a - 2] = back_transpose(c_t[a - 2], bank("c0"), 0, 4)
        act_gate(a, 0, nxt[0], 0, 512)
        act_gate(a, 1, nxt[1], 0, 512)
        cmult(nc.gpsimd, a, 0, 512)
        zz = [mx_pass(z, gi, 0, 512) for gi in range(3)]
        act_c(a - 2, c_ps[a - 2], 0, 512)
        c_ps[a - 1] = back_transpose(c_t[a - 1], bank("in0"), 0, 4)
        o_ps[a - 1] = back_transpose(acts[(a - 1, 2)], bank("o%d" % ((a - 1) % 2)), 0, 4)
        act_gate(z, 0, zz[0], 0, 512)
        act_gate(z, 1, zz[1], 0, 256)
        act_gate(z, 1, zz[1], 256, 512, 256)
        act_c(a - 1, c_ps[a - 1], 0, 512)
        act_gate(a, 2, nxt[2], 0, 512)
        final(a - 2, 0, 4)
        store_unit(a - 2, 0, 4)
        cmult(nc.vector, z, 0, 256)
        cmult(nc.vector, z, 256, 512)
        final(a - 1, 0, 4)
        store_unit(a - 1, 0, 4)
        c_ps[a] = back_transpose(c_t[a], bank("c0"), 0, 4)
        c_lo = back_transpose(c_t[z], bank("m3"), 0, 2)
        c_hi = back_transpose(c_t[z], bank("m0"), 2, 4)
        o_ps[a] = back_transpose(acts[(a, 2)], bank("o%d" % (a % 2)), 0, 4)
        act_c(a, c_ps[a], 0, 512)
        act_gate(z, 2, zz[2], 0, 256)
        act_gate(z, 2, zz[2], 256, 512, 256)
        final(a, 0, 4)
        store_unit(a, 0, 4)
        o_lo = back_transpose(acts[(z, 2)], bank("in0"), 0, 2)
        o_hi = back_transpose(acts[(z, 2)], bank("m2"), 2, 4)
        act_c(z, c_lo, 0, 256)
        act_c(z, c_hi, 256, 384)
        act_c(z, c_hi, 384, 512, 128)
        for t0, t1, ps, first in ((0, 2, o_lo, 0), (2, 3, o_hi, 2), (3, 4, o_hi, 2)):
            final(z, t0, t1, ps, first)
            store_unit(z, t0, t1)
